import numpy as np
import ml_dtypes


def mxq(x, axis, fmt="e4m3"):
    dtype, down = {"e4m3": (ml_dtypes.float8_e4m3fn, 7), "e5m2": (ml_dtypes.float8_e5m2, 14)}[fmt]
    v = np.moveaxis(np.asarray(x, np.float32).astype(ml_dtypes.bfloat16).astype(np.float64), axis, -1)
    blocks = v.reshape(v.shape[:-1] + (-1, 32))
    amax = np.abs(blocks).max(-1, keepdims=True)
    byte = np.maximum(np.where(amax > 0, np.frexp(amax)[1] - 1 + 127, 0) - down, 1)
    scale = np.exp2(byte - 127.0)
    codes = (blocks / scale).astype(np.float32).astype(dtype).astype(np.float64)
    return np.moveaxis((codes * scale).reshape(v.shape), -1, axis)


WIDE = False


def mx_kscale(k):
    if not WIDE:
        return np.ones(k)
    levels = np.array([10, -10, 5, -5, 0])
    a = np.random.permutation(np.resize(levels, k // 512 * 4)).reshape(k // 512, 4)
    idx = np.arange(k)
    return np.exp2(a[idx // 512, idx % 128 // 32])


BF16 = ml_dtypes.bfloat16


def bf(x):
    return np.asarray(x, np.float32).astype(BF16)


def f64(x):
    return np.asarray(x).astype(np.float64)


B, N_I, N_H1, N_H2, N_H3, N_H4 = 512, 1024, 1024, 1024, 2048, 1024
K1 = N_I + N_H1


def sigmoid(v):
    return 1.0 / (1.0 + np.exp(-v))


def setup_inputs():
    s = mx_kscale(K1)

    def w(gain):
        return bf(np.random.standard_normal((N_H1, K1)) * gain / np.sqrt(K1) / s[None, :])

    def b():
        return bf(np.random.standard_normal(N_H1) * 0.3)

    return {"X": bf(np.random.standard_normal((B, N_I)) * s[:N_I]),
            "hidden1": bf(np.random.standard_normal((B, N_H1)) * s[N_I:]),
            "cell1": bf(np.random.standard_normal((B, N_H1))),
            "Wf1": w(1.0), "bf1": b(), "Wi1": w(1.0), "bi1": b(),
            "Wc1": w(5.0 / 3.0), "bc1": b(), "Wo1": w(1.0), "bo1": b()}


def reference(X, hidden1, cell1, Wf1, bf1, Wi1, bi1, Wc1, bc1, Wo1, bo1):
    zq = mxq(np.concatenate([f64(X), f64(hidden1)], axis=1), 1, "e4m3")
    f = sigmoid((zq @ mxq(f64(Wf1), 1, "e4m3").T) + f64(bf1))
    i = sigmoid((zq @ mxq(f64(Wi1), 1, "e4m3").T) + f64(bi1))
    cand = np.tanh((zq @ mxq(f64(Wc1), 1, "e4m3").T) + f64(bc1))
    o = sigmoid((zq @ mxq(f64(Wo1), 1, "e4m3").T) + f64(bo1))
    h_new = o * np.tanh(cand)
    c_new = f * f64(cell1) + cand * i
    return h_new, c_new

@@ -1,0 +1,286 @@
+from contextlib import ExitStack
+
+import concourse.mybir as mybir
+from concourse.masks import make_identity
+
+FP8X4 = mybir.dt.float8_e4m3fn_x4
+BF16 = mybir.dt.bfloat16
+F32 = mybir.dt.float32
+U32 = mybir.dt.uint32
+U8 = mybir.dt.uint8
+ACT = mybir.ActivationFunctionType
+ALU = mybir.AluOpType
+
+P = 128
+BATCH = 512
+N_IN = 1024
+N_HID = 1024
+K = N_IN + N_HID
+PACK = 4
+K_PASS = P * PACK
+PASSES = K // K_PASS
+BANK = 512
+
+SLAB_ROWS = 256
+ROW_TILES = SLAB_ROWS // P
+SLAB_WORDS = PASSES * SLAB_ROWS
+Z_SLABS = BATCH // SLAB_ROWS
+CHUNKS = N_HID // SLAB_ROWS
+GATES = ("c", "i", "f", "o")
+W_SLABS = CHUNKS * len(GATES)
+RAW_BUFS = 8
+QUANT_CALLS = 2
+
+FLOPS = 2 * BATCH * len(GATES) * N_HID * K
+
+
+def tile_quest_pa_kernel(
+    tc, X, hidden1, cell1, Wf1, bf1, Wi1, bi1, Wc1, bc1, Wo1, bo1, out_0, out_1
+):
+    nc = tc.nc
+    weight = {"f": Wf1, "i": Wi1, "c": Wc1, "o": Wo1}
+    bias = {"f": bf1, "i": bi1, "c": bc1, "o": bo1}
+    h_rows = out_0.rearrange("(t p) n -> p t n", p=P)
+    c_rows = out_1.rearrange("(t p) n -> p t n", p=P)
+
+    with ExitStack() as ctx:
+        const = ctx.enter_context(tc.tile_pool(name="const", bufs=1))
+        raw_pool = ctx.enter_context(tc.tile_pool(name="raw", bufs=RAW_BUFS))
+        grouped_pool = ctx.enter_context(tc.tile_pool(name="grouped", bufs=2))
+        w_pool = ctx.enter_context(tc.tile_pool(name="w_mx", bufs=3))
+        gate_pool = ctx.enter_context(tc.tile_pool(name="gates", bufs=2))
+        turn_pool = ctx.enter_context(tc.psum_pool(name="turned", bufs=4))
+        acc_pool = ctx.enter_context(tc.psum_pool(name="acc", bufs=4))
+        ctx.enter_context(tc.manual_schedule())
+
+        def load_slab(q):
+            raw = raw_pool.tile([P, ROW_TILES * K], BF16, name="raw", tag="raw")
+            raw_rows = raw[:].rearrange("p (a k) -> p a k", a=ROW_TILES)
+            if q < Z_SLABS:
+                rows = slice(q * SLAB_ROWS, (q + 1) * SLAB_ROWS)
+                nc.sync.dma_start(
+                    out=raw_rows[:, :, 0:N_IN],
+                    in_=X[rows, :].rearrange("(a p) k -> p a k", p=P),
+                )
+                nc.sync.dma_start(
+                    out=raw_rows[:, :, N_IN:K],
+                    in_=hidden1[rows, :].rearrange("(a p) k -> p a k", p=P),
+                )
+            else:
+                chunk, gate = divmod(q - Z_SLABS, len(GATES))
+                rows = slice(chunk * SLAB_ROWS, (chunk + 1) * SLAB_ROWS)
+                nc.sync.dma_start(
+                    out=raw_rows,
+                    in_=weight[GATES[gate]][rows, :].rearrange("(a p) k -> p a k", p=P),
+                )
+            return raw
+
+        def turn_slab(raw):
+            raw_words = raw[:].bitcast(F32)
+            grouped = grouped_pool.tile(
+                [P, SLAB_WORDS * PACK], BF16, name="grouped", tag="grouped", align_bytes=64
+            )
+            grouped_words = grouped[:].bitcast(F32)
+            for g in range(PASSES):
+                turned = turn_pool.tile([P, BANK], F32, name="turned", tag="turned")
+                for a in range(ROW_TILES):
+                    for u in range(2):
+                        first = a * (K // 2) + g * (K_PASS // 2) + u * P
+                        place = (2 * a + u) * P
+                        nc.tensor.transpose(
+                            turned[:, place : place + P], raw_words[:, first : first + P], ident[:]
+                        )
+                nc.scalar.copy(
+                    out=grouped_words[:, g * BANK : (g + 1) * BANK].rearrange(
+                        "p (a r u) -> p a r u", a=ROW_TILES, u=2
+                    ),
+                    in_=turned[:].rearrange("p (a u r) -> p a r u", a=ROW_TILES, u=2),
+                )
+            return grouped
+
+        def quantise_slab(grouped, codes, scales):
+            words = SLAB_WORDS // QUANT_CALLS
+            for call in range(QUANT_CALLS):
+                nc.vector.quantize_mx(
+                    out=codes[:, call * words : (call + 1) * words].bitcast(FP8X4),
+                    scales=scales[:, call * words : (call + 1) * words],
+                    in_=grouped[:, call * words * PACK : (call + 1) * words * PACK],
+                )
+
+        def spread_bias(gate):
+            for half in range(N_HID // BANK):
+                cols = slice(gate * N_HID + half * BANK, gate * N_HID + (half + 1) * BANK)
+                spread = acc_pool.tile([P, BANK], F32, name="spread", tag="acc")
+                nc.tensor.matmul(
+                    out=spread[:], lhsT=ones[:], rhs=bias_rows[:, cols], start=True, stop=True
+                )
+                nc.vector.tensor_copy(out=bias_all[:, cols], in_=spread[:])
+
+        def multiply_slab(codes, scales):
+            banks = []
+            for pair in range(Z_SLABS):
+                acc = acc_pool.tile([P, BANK], F32, name="acc", tag="acc")
+                for a in range(ROW_TILES):
+                    for g in range(PASSES):
+                        z_cols = slice(g * SLAB_ROWS + a * P, g * SLAB_ROWS + (a + 1) * P)
+                        w_cols = slice(g * SLAB_ROWS, (g + 1) * SLAB_ROWS)
+                        nc.tensor.matmul_mx(
+                            out=acc[:, a * SLAB_ROWS : (a + 1) * SLAB_ROWS],
+                            lhsT=z_codes[pair][:, z_cols].bitcast(FP8X4),
+                            lhsT_scale=z_scales[pair][:, z_cols],
+                            rhs=codes[:, w_cols].bitcast(FP8X4),
+                            rhs_scale=scales[:, w_cols],
+                            start=(g == 0),
+                            stop=(g == PASSES - 1),
+                        )
+                banks.append(acc)
+            return banks
+
+        def add_bias(s, banks):
+            chunk, gate = divmod(s, len(GATES))
+            first = gate * N_HID + chunk * SLAB_ROWS
+            value = gate_pool.tile(
+                [P, Z_SLABS * BANK], F32, name="gate_" + GATES[gate], tag="gate_" + GATES[gate]
+            )
+            for pair in range(Z_SLABS):
+                nc.vector.tensor_tensor(
+                    out=value[:, pair * BANK : (pair + 1) * BANK].rearrange(
+                        "p (a n) -> p a n", a=ROW_TILES
+                    ),
+                    in0=banks[pair][:].rearrange("p (a n) -> p a n", a=ROW_TILES),
+                    in1=bias_all[:, first : first + SLAB_ROWS]
+                    .unsqueeze(1)
+                    .to_broadcast([P, ROW_TILES, SLAB_ROWS]),
+                    op=ALU.add,
+                )
+            return value
+
+        def activate(s, value):
+            gate = GATES[s % len(GATES)]
+            for pair in range(Z_SLABS):
+                cols = slice(pair * BANK, (pair + 1) * BANK)
+                nc.scalar.activation(
+                    out=value[:, cols],
+                    in_=value[:, cols],
+                    func=ACT.Tanh if gate == "c" else ACT.Sigmoid,
+                )
+            if gate != "c":
+                return None
+            squashed = gate_pool.tile([P, Z_SLABS * BANK], F32, name="squashed", tag="squashed")
+            for pair in range(Z_SLABS):
+                cols = slice(pair * BANK, (pair + 1) * BANK)
+                nc.scalar.activation(out=squashed[:, cols], in_=value[:, cols], func=ACT.Tanh)
+            return squashed
+
+        def combine(step):
+            chunk, kind = divmod(step, 4)
+            out_cols = slice(chunk * SLAB_ROWS, (chunk + 1) * SLAB_ROWS)
+            for pair in range(Z_SLABS):
+                cols = slice(pair * BANK, (pair + 1) * BANK)
+                tiles = slice(pair * ROW_TILES, (pair + 1) * ROW_TILES)
+                if kind == 0:
+                    nc.vector.tensor_tensor(
+                        out=values[chunk, "i"][:, cols],
+                        in0=values[chunk, "i"][:, cols],
+                        in1=values[chunk, "c"][:, cols],
+                        op=ALU.mult,
+                    )
+                elif kind == 1:
+                    nc.vector.tensor_tensor(
+                        out=values[chunk, "f"][:, cols].rearrange("p (a n) -> p a n", a=ROW_TILES),
+                        in0=values[chunk, "f"][:, cols].rearrange("p (a n) -> p a n", a=ROW_TILES),
+                        in1=cell_rows[:, tiles, out_cols],
+                        op=ALU.mult,
+                    )
+                elif kind == 2:
+                    nc.vector.tensor_tensor(
+                        out=values[chunk, "f"][:, cols],
+                        in0=values[chunk, "f"][:, cols],
+                        in1=values[chunk, "i"][:, cols],
+                        op=ALU.add,
+                    )
+                    nc.sync.dma_start(
+                        out=c_rows[:, tiles, out_cols],
+                        in_=values[chunk, "f"][:, cols].rearrange("p (a n) -> p a n", a=ROW_TILES),
+                    )
+                else:
+                    nc.vector.tensor_tensor(
+                        out=values[chunk, "o"][:, cols],
+                        in0=values[chunk, "o"][:, cols],
+                        in1=values[chunk, "tanh_c"][:, cols],
+                        op=ALU.mult,
+                    )
+                    nc.sync.dma_start(
+                        out=h_rows[:, tiles, out_cols],
+                        in_=values[chunk, "o"][:, cols].rearrange("p (a n) -> p a n", a=ROW_TILES),
+                    )
+
+        raws = {}
+        for q in range(RAW_BUFS):
+            raws[q] = load_slab(q)
+        cell_sb = const.tile([P, (BATCH // P) * N_HID], BF16, name="cell_sb")
+        cell_rows = cell_sb[:].rearrange("p (t n) -> p t n", n=N_HID)
+        nc.sync.dma_start(out=cell_rows, in_=cell1.rearrange("(t p) n -> p t n", p=P))
+
+        ident = const.tile([P, P], F32, name="ident")
+        make_identity(nc, ident[:])
+        ones = const.tile([P, P], BF16, name="ones")
+        nc.vector.memset(ones[:], 1.0)
+        bias_rows = const.tile([P, len(GATES) * N_HID], BF16, name="bias_rows")
+        nc.vector.memset(bias_rows[:].bitcast(F32), 0.0)
+        for gate in range(len(GATES)):
+            nc.scalar.dma_start(
+                out=bias_rows[0:1, gate * N_HID : (gate + 1) * N_HID],
+                in_=bias[GATES[gate]].rearrange("(o n) -> o n", o=1),
+            )
+        bias_all = const.tile([P, len(GATES) * N_HID], F32, name="bias_all")
+        warm = const.tile([P, 1], F32, name="warm")
+        nc.vector.memset(warm[:], 0.0)
+        nc.scalar.activation(out=warm[:], in_=warm[:], func=ACT.Sigmoid)
+
+        z_codes = []
+        z_scales = []
+        for pair in range(Z_SLABS):
+            z_codes.append(
+                const.tile([P, SLAB_WORDS], U32, name="z_codes%d" % pair, align_bytes=64)
+            )
+            z_scales.append(
+                const.tile([P, SLAB_WORDS], U8, name="z_scales%d" % pair, align_bytes=64)
+            )
+
+        mx = {}
+        sums = {}
+        values = {}
+        next_step = 0
+        for s in range(-Z_SLABS - 1, W_SLABS + 1):
+            turning = s + 1 < W_SLABS
+            if turning:
+                q = s + 1 + Z_SLABS
+                grouped = turn_slab(raws[q])
+                if q + RAW_BUFS < Z_SLABS + W_SLABS:
+                    raws[q + RAW_BUFS] = load_slab(q + RAW_BUFS)
+            if s < len(GATES) - Z_SLABS - 1:
+                spread_bias(s + Z_SLABS + 1)
+            if s >= 3:
+                combine(next_step)
+                next_step += 1
+            if 0 <= s - 1:
+                chunk, gate = divmod(s - 1, len(GATES))
+                values[chunk, GATES[gate]] = add_bias(s - 1, sums[s - 1])
+                squashed = activate(s - 1, values[chunk, GATES[gate]])
+                if squashed is not None:
+                    values[chunk, "tanh_c"] = squashed
+            if turning:
+                if s + 1 < 0:
+                    codes, scales = z_codes[s + 1 + Z_SLABS], z_scales[s + 1 + Z_SLABS]
+                else:
+                    codes = w_pool.tile([P, SLAB_WORDS], U32, name="codes", tag="codes", align_bytes=64)
+                    scales = w_pool.tile([P, SLAB_WORDS], U8, name="scales", tag="scales", align_bytes=64)
+                    mx[s + 1] = (codes, scales)
+                quantise_slab(grouped, codes, scales)
+            else:
+                combine(next_step)
+                next_step += 1
+            if 0 <= s < W_SLABS:
+                codes, scales = mx[s]
+                sums[s] = multiply_slab(codes, scales)

@@ -30,6 +30,7 @@ GATES = ("c", "i", "f", "o")
 W_SLABS = CHUNKS * len(GATES)
 RAW_BUFS = 8
 QUANT_CALLS = 2
+SCALAR_BANKS = 3
 
 FLOPS = 2 * BATCH * len(GATES) * N_HID * K
 
@@ -90,12 +91,14 @@ def tile_quest_pa_kernel(
                         nc.tensor.transpose(
                             turned[:, place : place + P], raw_words[:, first : first + P], ident[:]
                         )
-                nc.scalar.copy(
-                    out=grouped_words[:, g * BANK : (g + 1) * BANK].rearrange(
-                        "p (a r u) -> p a r u", a=ROW_TILES, u=2
-                    ),
-                    in_=turned[:].rearrange("p (a u r) -> p a r u", a=ROW_TILES, u=2),
+                side_by_side = grouped_words[:, g * BANK : (g + 1) * BANK].rearrange(
+                    "p (a r u) -> p a r u", a=ROW_TILES, u=2
                 )
+                as_turned = turned[:].rearrange("p (a u r) -> p a r u", a=ROW_TILES, u=2)
+                if g < SCALAR_BANKS:
+                    nc.scalar.copy(out=side_by_side, in_=as_turned)
+                else:
+                    nc.vector.tensor_copy(out=side_by_side, in_=as_turned)
             return grouped
 
         def quantise_slab(grouped, codes, scales):
@@ -172,28 +175,27 @@ def tile_quest_pa_kernel(
                 nc.scalar.activation(out=squashed[:, cols], in_=value[:, cols], func=ACT.Tanh)
             return squashed
 
-        def combine(step):
-            chunk, kind = divmod(step, 4)
+        def combine(s):
+            chunk, gate = divmod(s, len(GATES))
             out_cols = slice(chunk * SLAB_ROWS, (chunk + 1) * SLAB_ROWS)
             for pair in range(Z_SLABS):
                 cols = slice(pair * BANK, (pair + 1) * BANK)
                 tiles = slice(pair * ROW_TILES, (pair + 1) * ROW_TILES)
-                if kind == 0:
-                    nc.vector.tensor_tensor(
+                if GATES[gate] == "i":
+                    nc.gpsimd.tensor_tensor(
                         out=values[chunk, "i"][:, cols],
                         in0=values[chunk, "i"][:, cols],
                         in1=values[chunk, "c"][:, cols],
                         op=ALU.mult,
                     )
-                elif kind == 1:
-                    nc.vector.tensor_tensor(
+                elif GATES[gate] == "f":
+                    nc.gpsimd.tensor_tensor(
                         out=values[chunk, "f"][:, cols].rearrange("p (a n) -> p a n", a=ROW_TILES),
                         in0=values[chunk, "f"][:, cols].rearrange("p (a n) -> p a n", a=ROW_TILES),
                         in1=cell_rows[:, tiles, out_cols],
                         op=ALU.mult,
                     )
-                elif kind == 2:
-                    nc.vector.tensor_tensor(
+                    nc.gpsimd.tensor_tensor(
                         out=values[chunk, "f"][:, cols],
                         in0=values[chunk, "f"][:, cols],
                         in1=values[chunk, "i"][:, cols],
@@ -203,8 +205,8 @@ def tile_quest_pa_kernel(
                         out=c_rows[:, tiles, out_cols],
                         in_=values[chunk, "f"][:, cols].rearrange("p (a n) -> p a n", a=ROW_TILES),
                     )
-                else:
-                    nc.vector.tensor_tensor(
+                elif GATES[gate] == "o":
+                    nc.gpsimd.tensor_tensor(
                         out=values[chunk, "o"][:, cols],
                         in0=values[chunk, "o"][:, cols],
                         in1=values[chunk, "tanh_c"][:, cols],
@@ -251,9 +253,12 @@ def tile_quest_pa_kernel(
         mx = {}
         sums = {}
         values = {}
-        next_step = 0
         for s in range(-Z_SLABS - 1, W_SLABS + 1):
             turning = s + 1 < W_SLABS
+            finishing = 0 <= s - 1
+            if finishing:
+                chunk, gate = divmod(s - 1, len(GATES))
+                values[chunk, GATES[gate]] = add_bias(s - 1, sums[s - 1])
             if turning:
                 q = s + 1 + Z_SLABS
                 grouped = turn_slab(raws[q])
@@ -261,15 +266,11 @@ def tile_quest_pa_kernel(
                     raws[q + RAW_BUFS] = load_slab(q + RAW_BUFS)
             if s < len(GATES) - Z_SLABS - 1:
                 spread_bias(s + Z_SLABS + 1)
-            if s >= 3:
-                combine(next_step)
-                next_step += 1
-            if 0 <= s - 1:
-                chunk, gate = divmod(s - 1, len(GATES))
-                values[chunk, GATES[gate]] = add_bias(s - 1, sums[s - 1])
+            if finishing:
                 squashed = activate(s - 1, values[chunk, GATES[gate]])
                 if squashed is not None:
                     values[chunk, "tanh_c"] = squashed
+                combine(s - 1)
             if turning:
                 if s + 1 < 0:
                     codes, scales = z_codes[s + 1 + Z_SLABS], z_scales[s + 1 + Z_SLABS]
@@ -278,9 +279,6 @@ def tile_quest_pa_kernel(
                     scales = w_pool.tile([P, SLAB_WORDS], U8, name="scales", tag="scales", align_bytes=64)
                     mx[s + 1] = (codes, scales)
                 quantise_slab(grouped, codes, scales)
-            else:
-                combine(next_step)
-                next_step += 1
             if 0 <= s < W_SLABS:
                 codes, scales = mx[s]
                 sums[s] = multiply_slab(codes, scales)

@@ -189,7 +189,7 @@ def tile_quest_pa_kernel(
                         op=ALU.mult,
                     )
                 elif GATES[gate] == "f":
-                    nc.gpsimd.tensor_tensor(
+                    nc.vector.tensor_tensor(
                         out=values[chunk, "f"][:, cols].rearrange("p (a n) -> p a n", a=ROW_TILES),
                         in0=values[chunk, "f"][:, cols].rearrange("p (a n) -> p a n", a=ROW_TILES),
                         in1=cell_rows[:, tiles, out_cols],
@@ -206,7 +206,7 @@ def tile_quest_pa_kernel(
                         in_=values[chunk, "f"][:, cols].rearrange("p (a n) -> p a n", a=ROW_TILES),
                     )
                 elif GATES[gate] == "o":
-                    nc.gpsimd.tensor_tensor(
+                    nc.vector.tensor_tensor(
                         out=values[chunk, "o"][:, cols],
                         in0=values[chunk, "o"][:, cols],
                         in1=values[chunk, "tanh_c"][:, cols],
@@ -270,7 +270,6 @@ def tile_quest_pa_kernel(
                 squashed = activate(s - 1, values[chunk, GATES[gate]])
                 if squashed is not None:
                     values[chunk, "tanh_c"] = squashed
-                combine(s - 1)
             if turning:
                 if s + 1 < 0:
                     codes, scales = z_codes[s + 1 + Z_SLABS], z_scales[s + 1 + Z_SLABS]
@@ -279,6 +278,8 @@ def tile_quest_pa_kernel(
                     scales = w_pool.tile([P, SLAB_WORDS], U8, name="scales", tag="scales", align_bytes=64)
                     mx[s + 1] = (codes, scales)
                 quantise_slab(grouped, codes, scales)
+            if finishing:
+                combine(s - 1)
             if 0 <= s < W_SLABS:
                 codes, scales = mx[s]
                 sums[s] = multiply_slab(codes, scales)

from contextlib import ExitStack

import concourse.mybir as mybir
from concourse.masks import make_identity

FP8X4 = mybir.dt.float8_e4m3fn_x4
BF16 = mybir.dt.bfloat16
F32 = mybir.dt.float32
U32 = mybir.dt.uint32
U8 = mybir.dt.uint8
ACT = mybir.ActivationFunctionType
ALU = mybir.AluOpType

P = 128
BATCH = 512
N_IN = 1024
N_HID = 1024
K = N_IN + N_HID
PACK = 4
K_PASS = P * PACK
PASSES = K // K_PASS
BANK = 512

SLAB_ROWS = 256
ROW_TILES = SLAB_ROWS // P
SLAB_WORDS = PASSES * SLAB_ROWS
Z_SLABS = BATCH // SLAB_ROWS
CHUNKS = N_HID // SLAB_ROWS
GATES = ("c", "i", "f", "o")
W_SLABS = CHUNKS * len(GATES)
RAW_BUFS = 8
QUANT_CALLS = 2
SCALAR_BANKS = 3

FLOPS = 2 * BATCH * len(GATES) * N_HID * K


def tile_quest_pa_kernel(
    tc, X, hidden1, cell1, Wf1, bf1, Wi1, bi1, Wc1, bc1, Wo1, bo1, out_0, out_1
):
    nc = tc.nc
    weight = {"f": Wf1, "i": Wi1, "c": Wc1, "o": Wo1}
    bias = {"f": bf1, "i": bi1, "c": bc1, "o": bo1}
    h_rows = out_0.rearrange("(t p) n -> p t n", p=P)
    c_rows = out_1.rearrange("(t p) n -> p t n", p=P)

    with ExitStack() as ctx:
        const = ctx.enter_context(tc.tile_pool(name="const", bufs=1))
        raw_pool = ctx.enter_context(tc.tile_pool(name="raw", bufs=RAW_BUFS))
        grouped_pool = ctx.enter_context(tc.tile_pool(name="grouped", bufs=2))
        w_pool = ctx.enter_context(tc.tile_pool(name="w_mx", bufs=3))
        gate_pool = ctx.enter_context(tc.tile_pool(name="gates", bufs=2))
        turn_pool = ctx.enter_context(tc.psum_pool(name="turned", bufs=4))
        acc_pool = ctx.enter_context(tc.psum_pool(name="acc", bufs=4))
        ctx.enter_context(tc.manual_schedule())

        def load_slab(q):
            raw = raw_pool.tile([P, ROW_TILES * K], BF16, name="raw", tag="raw")
            raw_rows = raw[:].rearrange("p (a k) -> p a k", a=ROW_TILES)
            if q < Z_SLABS:
                rows = slice(q * SLAB_ROWS, (q + 1) * SLAB_ROWS)
                nc.sync.dma_start(
                    out=raw_rows[:, :, 0:N_IN],
                    in_=X[rows, :].rearrange("(a p) k -> p a k", p=P),
                )
                nc.sync.dma_start(
                    out=raw_rows[:, :, N_IN:K],
                    in_=hidden1[rows, :].rearrange("(a p) k -> p a k", p=P),
                )
            else:
                chunk, gate = divmod(q - Z_SLABS, len(GATES))
                rows = slice(chunk * SLAB_ROWS, (chunk + 1) * SLAB_ROWS)
                nc.sync.dma_start(
                    out=raw_rows,
                    in_=weight[GATES[gate]][rows, :].rearrange("(a p) k -> p a k", p=P),
                )
            return raw

        def turn_slab(raw):
            raw_words = raw[:].bitcast(F32)
            grouped = grouped_pool.tile(
                [P, SLAB_WORDS * PACK], BF16, name="grouped", tag="grouped", align_bytes=64
            )
            grouped_words = grouped[:].bitcast(F32)
            for g in range(PASSES):
                turned = turn_pool.tile([P, BANK], F32, name="turned", tag="turned")
                for a in range(ROW_TILES):
                    for u in range(2):
                        first = a * (K // 2) + g * (K_PASS // 2) + u * P
                        place = (2 * a + u) * P
                        nc.tensor.transpose(
                            turned[:, place : place + P], raw_words[:, first : first + P], ident[:]
                        )
                side_by_side = grouped_words[:, g * BANK : (g + 1) * BANK].rearrange(
                    "p (a r u) -> p a r u", a=ROW_TILES, u=2
                )
                as_turned = turned[:].rearrange("p (a u r) -> p a r u", a=ROW_TILES, u=2)
                if g < SCALAR_BANKS:
                    nc.scalar.copy(out=side_by_side, in_=as_turned)
                else:
                    nc.vector.tensor_copy(out=side_by_side, in_=as_turned)
            return grouped

        def quantise_slab(grouped, codes, scales):
            words = SLAB_WORDS // QUANT_CALLS
            for call in range(QUANT_CALLS):
                nc.vector.quantize_mx(
                    out=codes[:, call * words : (call + 1) * words].bitcast(FP8X4),
                    scales=scales[:, call * words : (call + 1) * words],
                    in_=grouped[:, call * words * PACK : (call + 1) * words * PACK],
                )

        def spread_bias(gate):
            for half in range(N_HID // BANK):
                cols = slice(gate * N_HID + half * BANK, gate * N_HID + (half + 1) * BANK)
                spread = acc_pool.tile([P, BANK], F32, name="spread", tag="acc")
                nc.tensor.matmul(
                    out=spread[:], lhsT=ones[:], rhs=bias_rows[:, cols], start=True, stop=True
                )
                nc.vector.tensor_copy(out=bias_all[:, cols], in_=spread[:])

        def multiply_slab(codes, scales):
            banks = []
            for pair in range(Z_SLABS):
                acc = acc_pool.tile([P, BANK], F32, name="acc", tag="acc")
                for a in range(ROW_TILES):
                    for g in range(PASSES):
                        z_cols = slice(g * SLAB_ROWS + a * P, g * SLAB_ROWS + (a + 1) * P)
                        w_cols = slice(g * SLAB_ROWS, (g + 1) * SLAB_ROWS)
                        nc.tensor.matmul_mx(
                            out=acc[:, a * SLAB_ROWS : (a + 1) * SLAB_ROWS],
                            lhsT=z_codes[pair][:, z_cols].bitcast(FP8X4),
                            lhsT_scale=z_scales[pair][:, z_cols],
                            rhs=codes[:, w_cols].bitcast(FP8X4),
                            rhs_scale=scales[:, w_cols],
                            start=(g == 0),
                            stop=(g == PASSES - 1),
                        )
                banks.append(acc)
            return banks

        def add_bias(s, banks):
            chunk, gate = divmod(s, len(GATES))
            first = gate * N_HID + chunk * SLAB_ROWS
            value = gate_pool.tile(
                [P, Z_SLABS * BANK], F32, name="gate_" + GATES[gate], tag="gate_" + GATES[gate]
            )
            for pair in range(Z_SLABS):
                nc.vector.tensor_tensor(
                    out=value[:, pair * BANK : (pair + 1) * BANK].rearrange(
                        "p (a n) -> p a n", a=ROW_TILES
                    ),
                    in0=banks[pair][:].rearrange("p (a n) -> p a n", a=ROW_TILES),
                    in1=bias_all[:, first : first + SLAB_ROWS]
                    .unsqueeze(1)
                    .to_broadcast([P, ROW_TILES, SLAB_ROWS]),
                    op=ALU.add,
                )
            return value

        def activate(s, value):
            gate = GATES[s % len(GATES)]
            for pair in range(Z_SLABS):
                cols = slice(pair * BANK, (pair + 1) * BANK)
                nc.scalar.activation(
                    out=value[:, cols],
                    in_=value[:, cols],
                    func=ACT.Tanh if gate == "c" else ACT.Sigmoid,
                )
            if gate != "c":
                return None
            squashed = gate_pool.tile([P, Z_SLABS * BANK], F32, name="squashed", tag="squashed")
            for pair in range(Z_SLABS):
                cols = slice(pair * BANK, (pair + 1) * BANK)
                nc.scalar.activation(out=squashed[:, cols], in_=value[:, cols], func=ACT.Tanh)
            return squashed

        def combine(s):
            chunk, gate = divmod(s, len(GATES))
            out_cols = slice(chunk * SLAB_ROWS, (chunk + 1) * SLAB_ROWS)
            for pair in range(Z_SLABS):
                cols = slice(pair * BANK, (pair + 1) * BANK)
                tiles = slice(pair * ROW_TILES, (pair + 1) * ROW_TILES)
                if GATES[gate] == "i":
                    nc.gpsimd.tensor_tensor(
                        out=values[chunk, "i"][:, cols],
                        in0=values[chunk, "i"][:, cols],
                        in1=values[chunk, "c"][:, cols],
                        op=ALU.mult,
                    )
                elif GATES[gate] == "f":
                    nc.vector.tensor_tensor(
                        out=values[chunk, "f"][:, cols].rearrange("p (a n) -> p a n", a=ROW_TILES),
                        in0=values[chunk, "f"][:, cols].rearrange("p (a n) -> p a n", a=ROW_TILES),
                        in1=cell_rows[:, tiles, out_cols],
                        op=ALU.mult,
                    )
                    nc.gpsimd.tensor_tensor(
                        out=values[chunk, "f"][:, cols],
                        in0=values[chunk, "f"][:, cols],
                        in1=values[chunk, "i"][:, cols],
                        op=ALU.add,
                    )
                    nc.sync.dma_start(
                        out=c_rows[:, tiles, out_cols],
                        in_=values[chunk, "f"][:, cols].rearrange("p (a n) -> p a n", a=ROW_TILES),
                    )
                elif GATES[gate] == "o":
                    nc.vector.tensor_tensor(
                        out=values[chunk, "o"][:, cols],
                        in0=values[chunk, "o"][:, cols],
                        in1=values[chunk, "tanh_c"][:, cols],
                        op=ALU.mult,
                    )
                    nc.sync.dma_start(
                        out=h_rows[:, tiles, out_cols],
                        in_=values[chunk, "o"][:, cols].rearrange("p (a n) -> p a n", a=ROW_TILES),
                    )

        raws = {}
        for q in range(RAW_BUFS):
            raws[q] = load_slab(q)
        cell_sb = const.tile([P, (BATCH // P) * N_HID], BF16, name="cell_sb")
        cell_rows = cell_sb[:].rearrange("p (t n) -> p t n", n=N_HID)
        nc.sync.dma_start(out=cell_rows, in_=cell1.rearrange("(t p) n -> p t n", p=P))

        ident = const.tile([P, P], F32, name="ident")
        make_identity(nc, ident[:])
        ones = const.tile([P, P], BF16, name="ones")
        nc.vector.memset(ones[:], 1.0)
        bias_rows = const.tile([P, len(GATES) * N_HID], BF16, name="bias_rows")
        nc.vector.memset(bias_rows[:].bitcast(F32), 0.0)
        for gate in range(len(GATES)):
            nc.scalar.dma_start(
                out=bias_rows[0:1, gate * N_HID : (gate + 1) * N_HID],
                in_=bias[GATES[gate]].rearrange("(o n) -> o n", o=1),
            )
        bias_all = const.tile([P, len(GATES) * N_HID], F32, name="bias_all")
        warm = const.tile([P, 1], F32, name="warm")
        nc.vector.memset(warm[:], 0.0)
        nc.scalar.activation(out=warm[:], in_=warm[:], func=ACT.Sigmoid)

        z_codes = []
        z_scales = []
        for pair in range(Z_SLABS):
            z_codes.append(
                const.tile([P, SLAB_WORDS], U32, name="z_codes%d" % pair, align_bytes=64)
            )
            z_scales.append(
                const.tile([P, SLAB_WORDS], U8, name="z_scales%d" % pair, align_bytes=64)
            )

        mx = {}
        sums = {}
        values = {}
        for s in range(-Z_SLABS - 1, W_SLABS + 1):
            turning = s + 1 < W_SLABS
            finishing = 0 <= s - 1
            if finishing:
                chunk, gate = divmod(s - 1, len(GATES))
                values[chunk, GATES[gate]] = add_bias(s - 1, sums[s - 1])
            if turning:
                q = s + 1 + Z_SLABS
                grouped = turn_slab(raws[q])
                if q + RAW_BUFS < Z_SLABS + W_SLABS:
                    raws[q + RAW_BUFS] = load_slab(q + RAW_BUFS)
            if s < len(GATES) - Z_SLABS - 1:
                spread_bias(s + Z_SLABS + 1)
            if finishing:
                squashed = activate(s - 1, values[chunk, GATES[gate]])
                if squashed is not None:
                    values[chunk, "tanh_c"] = squashed
            if turning:
                if s + 1 < 0:
                    codes, scales = z_codes[s + 1 + Z_SLABS], z_scales[s + 1 + Z_SLABS]
                else:
                    codes = w_pool.tile([P, SLAB_WORDS], U32, name="codes", tag="codes", align_bytes=64)
                    scales = w_pool.tile([P, SLAB_WORDS], U8, name="scales", tag="scales", align_bytes=64)
                    mx[s + 1] = (codes, scales)
                quantise_slab(grouped, codes, scales)
            if finishing:
                combine(s - 1)
            if 0 <= s < W_SLABS:
                codes, scales = mx[s]
                sums[s] = multiply_slab(codes, scales)
